import numpy as np
import ml_dtypes


def mxq(x, axis, fmt="e4m3"):
    dtype, down = {"e4m3": (ml_dtypes.float8_e4m3fn, 7), "e5m2": (ml_dtypes.float8_e5m2, 14)}[fmt]
    v = np.moveaxis(np.asarray(x, np.float32).astype(ml_dtypes.bfloat16).astype(np.float64), axis, -1)
    blocks = v.reshape(v.shape[:-1] + (-1, 32))
    amax = np.abs(blocks).max(-1, keepdims=True)
    byte = np.maximum(np.where(amax > 0, np.frexp(amax)[1] - 1 + 127, 0) - down, 1)
    scale = np.exp2(byte - 127.0)
    codes = (blocks / scale).astype(np.float32).astype(dtype).astype(np.float64)
    return np.moveaxis((codes * scale).reshape(v.shape), -1, axis)


WIDE = False


def mx_kscale(k):
    if not WIDE:
        return np.ones(k)
    levels = np.array([10, -10, 5, -5, 0])
    if k % 512:
        return np.exp2(np.random.permutation(np.resize(levels, k // 32))).repeat(32)
    a = np.empty((k // 512, 16))
    for p in range(k // 512):
        a[p, :8] = np.random.permutation(np.resize(levels, 8))
        for g in range(8):
            far = levels[np.abs(levels - a[p, g]) >= 10]
            a[p, g + 8] = far[np.random.randint(len(far))]
    return np.exp2(a.ravel()).repeat(32)


BF16 = ml_dtypes.bfloat16


def bf(x):
    return np.asarray(x, np.float32).astype(BF16)


def f64(x):
    return np.asarray(x).astype(np.float64)


N, C, T, V, H, QK = 1, 128, 128, 256, 4, 32
K = QK * V
MQ = np.sqrt(0.5 * np.sqrt(QK))


def setup_inputs():
    s = mx_kscale(K).reshape(QK, 1, V)
    q = MQ * np.random.standard_normal((N, H, QK, T, 1)) + 1.6 * np.random.standard_normal((N, H, QK, T, V))
    k = MQ * np.random.standard_normal((N, H, QK, T, 1)) + 1.6 * np.random.standard_normal((N, H, QK, T, V))
    return {"q": bf(q * s), "k": bf(k / s),
            "alphas": bf(0.2 * (1.0 + 0.3 * np.random.standard_normal((1, H, 1, 1)))),
            "att1s": bf(np.eye(T)[None, None] + 0.05 * np.random.standard_normal((1, H, T, T)))}


def reference(q, k, alphas, att1s):
    qf = np.swapaxes(f64(q), 2, 3).reshape(N, H, T, K)
    kf = np.swapaxes(f64(k), 2, 3).reshape(N, H, T, K)
    sc = mxq(qf, 3, "e4m3") @ np.swapaxes(mxq(kf, 3, "e4m3"), 2, 3)
    return np.tanh(sc / (QK * V)) * f64(alphas) + f64(att1s)

@@ -1,0 +1,175 @@
+from contextlib import ExitStack
+
+import concourse.mybir as mybir
+from concourse.masks import make_identity
+
+F32 = mybir.dt.float32
+BF16 = mybir.dt.bfloat16
+U32 = mybir.dt.uint32
+U8 = mybir.dt.uint8
+FP8X4 = mybir.dt.float8_e4m3fn_x4
+
+P = 128
+HEADS = 4
+CHANNELS = 32
+FRAMES = 128
+JOINTS = 256
+
+CHUNK_CHANNELS = 16
+CHUNKS_PER_HEAD = CHANNELS // CHUNK_CHANNELS
+PAIR = 2
+PASS_WORDS = PAIR * JOINTS // 2
+CHUNK_PASSES = CHUNK_CHANNELS // PAIR
+BANK_PASSES = 2
+TRANSPOSE_BANKS = 7
+CHUNK_COLUMNS = CHUNK_PASSES * FRAMES
+BURST_PASSES = 4
+BURSTS = CHUNK_PASSES // BURST_PASSES
+MOVING_COLUMNS = 256
+
+assert FRAMES == P and PASS_WORDS == 2 * P
+
+FLOPS = 2 * HEADS * FRAMES * FRAMES * CHANNELS * JOINTS
+
+
+def tile_model_pa_kernel(tc, q, k, alphas, att1s, out):
+    nc = tc.nc
+    rounds = [(h, c) for h in range(HEADS) for c in range(CHUNKS_PER_HEAD)]
+    with ExitStack() as ctx:
+        ctx.enter_context(tc.manual_schedule())
+        consts = ctx.enter_context(tc.tile_pool(name="consts", bufs=1))
+        raw_pool = ctx.enter_context(tc.tile_pool(name="raw", bufs=2 * len(rounds)))
+        grouped_pool = ctx.enter_context(tc.tile_pool(name="grouped", bufs=6))
+        mx_pool = ctx.enter_context(tc.tile_pool(name="mx", bufs=3))
+        result_pool = ctx.enter_context(tc.tile_pool(name="result", bufs=HEADS))
+        bank_pool = ctx.enter_context(tc.psum_pool(name="banks", bufs=TRANSPOSE_BANKS))
+        score_pool = ctx.enter_context(tc.psum_pool(name="scores", bufs=1))
+
+        raw_k = []
+        raw_q = []
+        for h, c in rounds:
+            for source, tiles in ((k, raw_k), (q, raw_q)):
+                raw = raw_pool.tile([P, CHUNK_CHANNELS * JOINTS], BF16)
+                pieces = 4 if (h, c) == rounds[-1] and source is q else 1
+                width = CHUNK_CHANNELS // pieces
+                for n in range(pieces):
+                    c0 = c * CHUNK_CHANNELS + n * width
+                    nc.sync.dma_start(
+                        out=raw[:, n * width * JOINTS : (n + 1) * width * JOINTS].rearrange(
+                            "t (c v) -> t c v", c=width
+                        ),
+                        in_=source[0, h, c0 : c0 + width].rearrange("c t v -> t c v"),
+                    )
+                tiles.append(raw)
+        alpha_bf16 = consts.tile([P, HEADS], BF16)
+        nc.sync.dma_start(
+            out=alpha_bf16[:], in_=alphas.rearrange("o h x y -> (o h x y)").partition_broadcast(P)
+        )
+        static_map = consts.tile([P, HEADS, FRAMES], BF16)
+        nc.sync.dma_start(out=static_map[:], in_=att1s[0].rearrange("h t u -> t h u"))
+
+        identity = consts.tile([P, P], F32)
+        make_identity(nc, identity[:])
+        table_warmer = consts.tile([P, 1], F32)
+        nc.scalar.activation(out=table_warmer[:], in_=identity[:, 0:1], func=mybir.ActivationFunctionType.Tanh)
+
+        k_columns = slice(0, CHUNK_COLUMNS)
+        q_columns = slice(CHUNK_COLUMNS, 2 * CHUNK_COLUMNS)
+        pending = []
+
+        def transposed(raw, codes, scales):
+            words = raw[:].bitcast(F32)
+            for n in range(BURSTS):
+                grouped = grouped_pool.tile([P, BURST_PASSES * FRAMES * 4], BF16, align_bytes=64)
+                grouped_words = grouped[:].bitcast(F32)
+                for i in range(BURST_PASSES // BANK_PASSES):
+                    bank = bank_pool.tile([P, BANK_PASSES * PAIR * FRAMES], F32)
+                    for j in range(BANK_PASSES * PAIR):
+                        g = n * BURST_PASSES + i * BANK_PASSES + j // PAIR
+                        s = j % PAIR
+                        nc.tensor.transpose(
+                            bank[:, j * FRAMES : (j + 1) * FRAMES],
+                            words[:, g * PASS_WORDS + s : (g + 1) * PASS_WORDS : PAIR],
+                            identity[:],
+                        )
+                    width = BANK_PASSES * PAIR * FRAMES
+                    to_grouped = grouped_words[:, i * width : (i + 1) * width].rearrange(
+                        "p (g t s) -> p g t s", g=BANK_PASSES, s=PAIR
+                    )
+                    from_bank = bank[:].rearrange("p (g s t) -> p g t s", g=BANK_PASSES, s=PAIR)
+                    if n == 0 and i == 1:
+                        nc.vector.tensor_copy(out=to_grouped, in_=from_bank)
+                    else:
+                        nc.scalar.copy(out=to_grouped, in_=from_bank)
+                while pending:
+                    pending.pop(0)()
+                columns = slice(n * BURST_PASSES * FRAMES, (n + 1) * BURST_PASSES * FRAMES)
+
+                def quantise(columns=columns, grouped=grouped):
+                    nc.vector.quantize_mx(
+                        out=codes[:, columns].bitcast(FP8X4), scales=scales[:, columns], in_=grouped[:]
+                    )
+
+                if n == 0:
+                    quantise()
+                else:
+                    pending.append(quantise)
+
+        def score_passes(scores, c, n, codes, scales):
+            for g in range(n * BURST_PASSES, (n + 1) * BURST_PASSES):
+                of_k = slice(g * FRAMES, g * FRAMES + MOVING_COLUMNS)
+                of_q = slice(CHUNK_COLUMNS + g * FRAMES, CHUNK_COLUMNS + (g + 1) * FRAMES)
+                nc.tensor.matmul_mx(
+                    out=scores[:],
+                    lhsT=codes[:, of_q].bitcast(FP8X4),
+                    lhsT_scale=scales[:, of_q],
+                    rhs=codes[:, of_k].bitcast(FP8X4),
+                    rhs_scale=scales[:, of_k],
+                    start=(c == 0 and g == 0),
+                    stop=(c == CHUNKS_PER_HEAD - 1 and g == CHUNK_PASSES - 1),
+                )
+
+        mx_tiles = {}
+        scores = None
+        squashed = []
+        for r in range(len(rounds) + 1):
+            if r < len(rounds):
+                codes = mx_pool.tile([P, 2 * CHUNK_COLUMNS], U32, align_bytes=64)
+                scales = mx_pool.tile([P, 2 * CHUNK_COLUMNS], U8, align_bytes=64)
+                mx_tiles[r] = (codes, scales)
+                transposed(raw_k[r], codes[:, k_columns], scales[:, k_columns])
+            else:
+                while pending:
+                    pending.pop(0)()
+            if r > 0:
+                h, c = rounds[r - 1]
+                if c == 0:
+                    scores = score_pool.tile([P, MOVING_COLUMNS], F32)
+                score_passes(scores, c, 0, *mx_tiles[r - 1])
+            if r < len(rounds):
+                transposed(raw_q[r], codes[:, q_columns], scales[:, q_columns])
+            if r > 0:
+                score_passes(scores, c, 1, *mx_tiles[r - 1])
+                if c == CHUNKS_PER_HEAD - 1:
+                    squashed_h = result_pool.tile([P, FRAMES], F32)
+                    nc.scalar.activation(
+                        out=squashed_h[:],
+                        in_=scores[:, 0:FRAMES],
+                        func=mybir.ActivationFunctionType.Tanh,
+                        scale=1.0 / (CHANNELS * JOINTS),
+                    )
+                    squashed.append(squashed_h)
+
+        alpha = consts.tile([P, HEADS], F32)
+        nc.vector.tensor_copy(out=alpha[:], in_=alpha_bf16[:])
+        for h in range(HEADS):
+            result = result_pool.tile([P, FRAMES], F32)
+            nc.vector.scalar_tensor_tensor(
+                out=result[:],
+                in0=squashed[h][:],
+                scalar=alpha[:, h : h + 1],
+                in1=static_map[:, h, :],
+                op0=mybir.AluOpType.mult,
+                op1=mybir.AluOpType.add,
+            )
+            nc.sync.dma_start(out=out[0, h], in_=result[:])

@@ -14,53 +14,50 @@ HEADS = 4
 CHANNELS = 32
 FRAMES = 128
 JOINTS = 256
-
-CHUNK_CHANNELS = 16
-CHUNKS_PER_HEAD = CHANNELS // CHUNK_CHANNELS
 PAIR = 2
-PASS_WORDS = PAIR * JOINTS // 2
-CHUNK_PASSES = CHUNK_CHANNELS // PAIR
-BANK_PASSES = 2
-TRANSPOSE_BANKS = 7
-CHUNK_COLUMNS = CHUNK_PASSES * FRAMES
+BLOCK = 32
+BLOCKS = JOINTS // BLOCK
+HALF = BLOCK // 2
+ROUND_CHANNELS = ((16, 16), (16, 16), (16, 16), (16, 8, 4, 4))
+TRANSPOSE_BANKS = 6
+MAX_COLUMNS = 8 * FRAMES
 BURST_PASSES = 4
-BURSTS = CHUNK_PASSES // BURST_PASSES
 MOVING_COLUMNS = 256
-
-assert FRAMES == P and PASS_WORDS == 2 * P
 
 FLOPS = 2 * HEADS * FRAMES * FRAMES * CHANNELS * JOINTS
 
 
 def tile_model_pa_kernel(tc, q, k, alphas, att1s, out):
     nc = tc.nc
-    rounds = [(h, c) for h in range(HEADS) for c in range(CHUNKS_PER_HEAD)]
+    rounds = []
+    for h in range(HEADS):
+        c0 = 0
+        for channels in ROUND_CHANNELS[h]:
+            rounds.append((h, c0, channels))
+            c0 += channels
     with ExitStack() as ctx:
         ctx.enter_context(tc.manual_schedule())
         consts = ctx.enter_context(tc.tile_pool(name="consts", bufs=1))
-        raw_pool = ctx.enter_context(tc.tile_pool(name="raw", bufs=2 * len(rounds)))
-        grouped_pool = ctx.enter_context(tc.tile_pool(name="grouped", bufs=6))
-        mx_pool = ctx.enter_context(tc.tile_pool(name="mx", bufs=3))
+        raw_pool = ctx.enter_context(tc.tile_pool(name="raw", bufs=1))
+        halves_pool = ctx.enter_context(tc.tile_pool(name="halves", bufs=3))
+        grouped_pool = ctx.enter_context(tc.tile_pool(name="grouped", bufs=3))
+        mx_pool = ctx.enter_context(tc.tile_pool(name="mx", bufs=4))
         result_pool = ctx.enter_context(tc.tile_pool(name="result", bufs=HEADS))
         bank_pool = ctx.enter_context(tc.psum_pool(name="banks", bufs=TRANSPOSE_BANKS))
-        score_pool = ctx.enter_context(tc.psum_pool(name="scores", bufs=1))
+        score_pool = ctx.enter_context(tc.psum_pool(name="scores", bufs=2))
 
-        raw_k = []
-        raw_q = []
-        for h, c in rounds:
-            for source, tiles in ((k, raw_k), (q, raw_q)):
-                raw = raw_pool.tile([P, CHUNK_CHANNELS * JOINTS], BF16)
-                pieces = 4 if (h, c) == rounds[-1] and source is q else 1
-                width = CHUNK_CHANNELS // pieces
-                for n in range(pieces):
-                    c0 = c * CHUNK_CHANNELS + n * width
-                    nc.sync.dma_start(
-                        out=raw[:, n * width * JOINTS : (n + 1) * width * JOINTS].rearrange(
-                            "t (c v) -> t c v", c=width
-                        ),
-                        in_=source[0, h, c0 : c0 + width].rearrange("c t v -> t c v"),
-                    )
-                tiles.append(raw)
+        chunks = []
+        for r, (h, c0, channels) in enumerate(rounds):
+            for source in (k, q):
+                raw = raw_pool.tile([P, channels * JOINTS], BF16, name="raw%d" % len(chunks))
+                passes = channels // PAIR
+                nc.sync.dma_start(
+                    out=raw[:].rearrange("p (e x) -> p e x", e=PAIR),
+                    in_=source[0, h, c0 : c0 + channels].rearrange(
+                        "(e c) (a b) v -> (c a) e (b v)", e=PAIR, a=P // passes
+                    ),
+                )
+                chunks.append((raw, r))
         alpha_bf16 = consts.tile([P, HEADS], BF16)
         nc.sync.dma_start(
             out=alpha_bf16[:], in_=alphas.rearrange("o h x y -> (o h x y)").partition_broadcast(P)
@@ -73,92 +70,114 @@ def tile_model_pa_kernel(tc, q, k, alphas, att1s, out):
         table_warmer = consts.tile([P, 1], F32)
         nc.scalar.activation(out=table_warmer[:], in_=identity[:, 0:1], func=mybir.ActivationFunctionType.Tanh)
 
-        k_columns = slice(0, CHUNK_COLUMNS)
-        q_columns = slice(CHUNK_COLUMNS, 2 * CHUNK_COLUMNS)
-        pending = []
+        mx_tiles = {}
+        halves_of = {}
+        grouped_of = {}
 
-        def transposed(raw, codes, scales):
-            words = raw[:].bitcast(F32)
-            for n in range(BURSTS):
-                grouped = grouped_pool.tile([P, BURST_PASSES * FRAMES * 4], BF16, align_bytes=64)
-                grouped_words = grouped[:].bitcast(F32)
-                for i in range(BURST_PASSES // BANK_PASSES):
-                    bank = bank_pool.tile([P, BANK_PASSES * PAIR * FRAMES], F32)
-                    for j in range(BANK_PASSES * PAIR):
-                        g = n * BURST_PASSES + i * BANK_PASSES + j // PAIR
-                        s = j % PAIR
-                        nc.tensor.transpose(
-                            bank[:, j * FRAMES : (j + 1) * FRAMES],
-                            words[:, g * PASS_WORDS + s : (g + 1) * PASS_WORDS : PAIR],
-                            identity[:],
-                        )
-                    width = BANK_PASSES * PAIR * FRAMES
-                    to_grouped = grouped_words[:, i * width : (i + 1) * width].rearrange(
-                        "p (g t s) -> p g t s", g=BANK_PASSES, s=PAIR
-                    )
-                    from_bank = bank[:].rearrange("p (g s t) -> p g t s", g=BANK_PASSES, s=PAIR)
-                    if n == 0 and i == 1:
-                        nc.vector.tensor_copy(out=to_grouped, in_=from_bank)
-                    else:
-                        nc.scalar.copy(out=to_grouped, in_=from_bank)
-                while pending:
-                    pending.pop(0)()
-                columns = slice(n * BURST_PASSES * FRAMES, (n + 1) * BURST_PASSES * FRAMES)
+        def split_halves(j):
+            raw, r = chunks[j]
+            b = rounds[r][2] // PAIR
+            halves = halves_pool.tile([P, 16 * JOINTS], BF16, name="halves")
+            to = halves[:, 0 : b * PAIR * JOINTS].rearrange(
+                "p (b x e i w) -> p x e b i w", b=b, x=2, e=PAIR, i=BLOCKS
+            )
+            of = raw[:].rearrange("p (e b i x w) -> p x e b i w", b=b, x=2, e=PAIR, i=BLOCKS)
+            for x in range(2):
+                for e in range(PAIR):
+                    nc.vector.tensor_copy(out=to[:, x, e], in_=of[:, x, e])
+            halves_of[j] = halves
 
-                def quantise(columns=columns, grouped=grouped):
-                    nc.vector.quantize_mx(
-                        out=codes[:, columns].bitcast(FP8X4), scales=scales[:, columns], in_=grouped[:]
-                    )
+        def transpose(j):
+            passes = rounds[chunks[j][1]][2] // PAIR
+            words = halves_of[j][:].bitcast(F32)
+            grouped = grouped_pool.tile([P, 8 * FRAMES * 4], BF16, align_bytes=64, name="grouped")
+            grouped_words = grouped[:, 0 : passes * FRAMES * 4].bitcast(F32).rearrange(
+                "p (c a n) -> p c a n", c=passes, a=P // passes
+            )
+            for i in range(passes // 2):
+                bank = bank_pool.tile([P, 4 * P], F32, name="bank")
+                for n in range(4):
+                    m = (i * 4 + n) * P
+                    nc.tensor.transpose(bank[:, n * P : (n + 1) * P], words[:, m : m + P], identity[:])
+                nc.scalar.copy(
+                    out=grouped_words[:, :, :, i * 4 : (i + 1) * 4],
+                    in_=bank[:].rearrange("p (n c a) -> p c a n", n=4, c=passes),
+                )
+            grouped_of[j] = grouped
 
-                if n == 0:
-                    quantise()
-                else:
-                    pending.append(quantise)
+        def quantise(j):
+            r = chunks[j][1]
+            passes = rounds[r][2] // PAIR
+            if j % 2 == 0:
+                codes = mx_pool.tile([P, 2 * MAX_COLUMNS], U32, align_bytes=64, name="codes")
+                scales = mx_pool.tile([P, 2 * MAX_COLUMNS], U8, align_bytes=64, name="scales")
+                mx_tiles[r] = (codes, scales)
+            codes, scales = mx_tiles[r]
+            first = (j % 2) * passes * FRAMES
+            step = min(passes, BURST_PASSES)
+            for g in range(0, passes, step):
+                columns = slice(first + g * FRAMES, first + (g + step) * FRAMES)
+                nc.vector.quantize_mx(
+                    out=codes[:, columns].bitcast(FP8X4),
+                    scales=scales[:, columns],
+                    in_=grouped_of[j][:, g * FRAMES * 4 : (g + step) * FRAMES * 4],
+                )
 
-        def score_passes(scores, c, n, codes, scales):
-            for g in range(n * BURST_PASSES, (n + 1) * BURST_PASSES):
+        scores_of = {}
+        squashed = {}
+
+        def score_passes(r, g0, g1):
+            h, c0, channels = rounds[r]
+            passes = channels // PAIR
+            if h not in scores_of:
+                scores_of[h] = score_pool.tile([P, MOVING_COLUMNS], F32, name="scores")
+            codes, scales = mx_tiles[r]
+            for g in range(g0, g1):
                 of_k = slice(g * FRAMES, g * FRAMES + MOVING_COLUMNS)
-                of_q = slice(CHUNK_COLUMNS + g * FRAMES, CHUNK_COLUMNS + (g + 1) * FRAMES)
+                of_q = slice((passes + g) * FRAMES, (passes + g + 1) * FRAMES)
                 nc.tensor.matmul_mx(
-                    out=scores[:],
+                    out=scores_of[h][:],
                     lhsT=codes[:, of_q].bitcast(FP8X4),
                     lhsT_scale=scales[:, of_q],
                     rhs=codes[:, of_k].bitcast(FP8X4),
                     rhs_scale=scales[:, of_k],
-                    start=(c == 0 and g == 0),
-                    stop=(c == CHUNKS_PER_HEAD - 1 and g == CHUNK_PASSES - 1),
+                    start=(c0 == 0 and g == 0),
+                    stop=(c0 + channels == CHANNELS and g == passes - 1),
                 )
 
-        mx_tiles = {}
-        scores = None
-        squashed = []
-        for r in range(len(rounds) + 1):
-            if r < len(rounds):
-                codes = mx_pool.tile([P, 2 * CHUNK_COLUMNS], U32, align_bytes=64)
-                scales = mx_pool.tile([P, 2 * CHUNK_COLUMNS], U8, align_bytes=64)
-                mx_tiles[r] = (codes, scales)
-                transposed(raw_k[r], codes[:, k_columns], scales[:, k_columns])
-            else:
-                while pending:
-                    pending.pop(0)()
-            if r > 0:
-                h, c = rounds[r - 1]
-                if c == 0:
-                    scores = score_pool.tile([P, MOVING_COLUMNS], F32)
-                score_passes(scores, c, 0, *mx_tiles[r - 1])
-            if r < len(rounds):
-                transposed(raw_q[r], codes[:, q_columns], scales[:, q_columns])
-            if r > 0:
-                score_passes(scores, c, 1, *mx_tiles[r - 1])
-                if c == CHUNKS_PER_HEAD - 1:
-                    squashed_h = result_pool.tile([P, FRAMES], F32)
-                    nc.scalar.activation(
-                        out=squashed_h[:],
-                        in_=scores[:, 0:FRAMES],
-                        func=mybir.ActivationFunctionType.Tanh,
-                        scale=1.0 / (CHANNELS * JOINTS),
-                    )
-                    squashed.append(squashed_h)
+        def squash(h):
+            squashed[h] = result_pool.tile([P, FRAMES], F32, name="squashed")
+            nc.scalar.activation(
+                out=squashed[h][:],
+                in_=scores_of[h][:, 0:FRAMES],
+                func=mybir.ActivationFunctionType.Tanh,
+                scale=1.0 / (CHANNELS * JOINTS),
+            )
+
+        steps = len(chunks)
+        to_squash = []
+        split_halves(0)
+        for j in range(steps + 3):
+            if j + 1 < steps:
+                split_halves(j + 1)
+            if j < steps:
+                transpose(j)
+            while to_squash:
+                squash(to_squash.pop(0))
+            if j < steps:
+                quantise(j)
+            if j >= 3:
+                r = (j - 3) // 2
+                h, c0, channels = rounds[r]
+                passes = channels // PAIR
+                if (j - 3) % 2 == 0:
+                    score_passes(r, 0, (passes + 1) // 2)
+                else:
+                    score_passes(r, (passes + 1) // 2, passes)
+                    if c0 + channels == CHANNELS:
+                        to_squash.append(h)
+        while to_squash:
+            squash(to_squash.pop(0))
 
         alpha = consts.tile([P, HEADS], F32)
         nc.vector.tensor_copy(out=alpha[:], in_=alpha_bf16[:])

@@ -39,7 +39,7 @@ def tile_model_pa_kernel(tc, q, k, alphas, att1s, out):
         ctx.enter_context(tc.manual_schedule())
         consts = ctx.enter_context(tc.tile_pool(name="consts", bufs=1))
         raw_pool = ctx.enter_context(tc.tile_pool(name="raw", bufs=1))
-        halves_pool = ctx.enter_context(tc.tile_pool(name="halves", bufs=3))
+        halves_pool = ctx.enter_context(tc.tile_pool(name="halves", bufs=4))
         grouped_pool = ctx.enter_context(tc.tile_pool(name="grouped", bufs=3))
         mx_pool = ctx.enter_context(tc.tile_pool(name="mx", bufs=4))
         result_pool = ctx.enter_context(tc.tile_pool(name="result", bufs=HEADS))
@@ -157,9 +157,10 @@ def tile_model_pa_kernel(tc, q, k, alphas, att1s, out):
         steps = len(chunks)
         to_squash = []
         split_halves(0)
+        split_halves(1)
         for j in range(steps + 3):
-            if j + 1 < steps:
-                split_halves(j + 1)
+            if j + 2 < steps:
+                split_halves(j + 2)
             if j < steps:
                 transpose(j)
             while to_squash:

@@ -18,7 +18,10 @@ PAIR = 2
 BLOCK = 32
 BLOCKS = JOINTS // BLOCK
 HALF = BLOCK // 2
-ROUND_CHANNELS = ((16, 16), (16, 16), (16, 16), (16, 8, 4, 4))
+ROUND_CHANNELS = ((16, 16), (16, 16), (16, 16), (16, 8, 8))
+BUFS = {16: 4, 8: 4}
+RAW_BUFS = {16: 9, 8: 4}
+AHEAD_CHANNELS = 32
 TRANSPOSE_BANKS = 6
 MAX_COLUMNS = 8 * FRAMES
 BURST_PASSES = 4
@@ -39,8 +42,8 @@ def tile_model_pa_kernel(tc, q, k, alphas, att1s, out):
         ctx.enter_context(tc.manual_schedule())
         consts = ctx.enter_context(tc.tile_pool(name="consts", bufs=1))
         raw_pool = ctx.enter_context(tc.tile_pool(name="raw", bufs=1))
-        halves_pool = ctx.enter_context(tc.tile_pool(name="halves", bufs=4))
-        grouped_pool = ctx.enter_context(tc.tile_pool(name="grouped", bufs=3))
+        halves_pool = ctx.enter_context(tc.tile_pool(name="halves", bufs=1))
+        grouped_pool = ctx.enter_context(tc.tile_pool(name="grouped", bufs=1))
         mx_pool = ctx.enter_context(tc.tile_pool(name="mx", bufs=4))
         result_pool = ctx.enter_context(tc.tile_pool(name="result", bufs=HEADS))
         bank_pool = ctx.enter_context(tc.psum_pool(name="banks", bufs=TRANSPOSE_BANKS))
@@ -49,7 +52,7 @@ def tile_model_pa_kernel(tc, q, k, alphas, att1s, out):
         chunks = []
         for r, (h, c0, channels) in enumerate(rounds):
             for source in (k, q):
-                raw = raw_pool.tile([P, channels * JOINTS], BF16, name="raw%d" % len(chunks))
+                raw = raw_pool.tile([P, channels * JOINTS], BF16, name="raw%d" % channels, bufs=RAW_BUFS[channels])
                 passes = channels // PAIR
                 nc.sync.dma_start(
                     out=raw[:].rearrange("p (e x) -> p e x", e=PAIR),
@@ -77,21 +80,22 @@ def tile_model_pa_kernel(tc, q, k, alphas, att1s, out):
         def split_halves(j):
             raw, r = chunks[j]
             b = rounds[r][2] // PAIR
-            halves = halves_pool.tile([P, 16 * JOINTS], BF16, name="halves")
-            to = halves[:, 0 : b * PAIR * JOINTS].rearrange(
+            halves = halves_pool.tile([P, 2 * b * JOINTS], BF16, name="halves%d" % b, bufs=BUFS[2 * b])
+            to = halves[:].rearrange(
                 "p (b x e i w) -> p x e b i w", b=b, x=2, e=PAIR, i=BLOCKS
             )
             of = raw[:].rearrange("p (e b i x w) -> p x e b i w", b=b, x=2, e=PAIR, i=BLOCKS)
             for x in range(2):
-                for e in range(PAIR):
-                    nc.vector.tensor_copy(out=to[:, x, e], in_=of[:, x, e])
+                nc.vector.tensor_copy(out=to[:, x], in_=of[:, x])
             halves_of[j] = halves
 
         def transpose(j):
             passes = rounds[chunks[j][1]][2] // PAIR
             words = halves_of[j][:].bitcast(F32)
-            grouped = grouped_pool.tile([P, 8 * FRAMES * 4], BF16, align_bytes=64, name="grouped")
-            grouped_words = grouped[:, 0 : passes * FRAMES * 4].bitcast(F32).rearrange(
+            grouped = grouped_pool.tile(
+                [P, passes * FRAMES * 4], BF16, align_bytes=64, name="grouped%d" % passes, bufs=BUFS[2 * passes]
+            )
+            grouped_words = grouped[:].bitcast(F32).rearrange(
                 "p (c a n) -> p c a n", c=passes, a=P // passes
             )
             for i in range(passes // 2):
@@ -155,28 +159,34 @@ def tile_model_pa_kernel(tc, q, k, alphas, att1s, out):
             )
 
         steps = len(chunks)
+        done = []
+        for raw, r in chunks:
+            done.append((done[-1] if done else 0) + rounds[r][2])
+        to_score = []
+        for r in range(len(rounds)):
+            passes = rounds[r][2] // PAIR
+            for n in range(2):
+                to_score.append(
+                    (done[2 * r + 1] + AHEAD_CHANNELS + n * 16, r, n * passes // 2, (n + 1) * passes // 2)
+                )
         to_squash = []
-        split_halves(0)
-        split_halves(1)
-        for j in range(steps + 3):
-            if j + 2 < steps:
-                split_halves(j + 2)
-            if j < steps:
+        split = 0
+        for j in range(-1, steps):
+            reached = done[j] if j >= 0 else 0
+            while split < steps and done[split] <= reached + AHEAD_CHANNELS:
+                split_halves(split)
+                split += 1
+            if j >= 0:
                 transpose(j)
-            while to_squash:
-                squash(to_squash.pop(0))
-            if j < steps:
+                while to_squash:
+                    squash(to_squash.pop(0))
                 quantise(j)
-            if j >= 3:
-                r = (j - 3) // 2
+            while to_score and (to_score[0][0] <= reached or j == steps - 1):
+                before, r, g0, g1 = to_score.pop(0)
+                score_passes(r, g0, g1)
                 h, c0, channels = rounds[r]
-                passes = channels // PAIR
-                if (j - 3) % 2 == 0:
-                    score_passes(r, 0, (passes + 1) // 2)
-                else:
-                    score_passes(r, (passes + 1) // 2, passes)
-                    if c0 + channels == CHANNELS:
-                        to_squash.append(h)
+                if c0 + channels == CHANNELS and g1 == channels // PAIR:
+                    to_squash.append(h)
         while to_squash:
             squash(to_squash.pop(0))
 

@@ -54,12 +54,14 @@ def tile_model_pa_kernel(tc, q, k, alphas, att1s, out):
             for source in (k, q):
                 raw = raw_pool.tile([P, channels * JOINTS], BF16, name="raw%d" % channels, bufs=RAW_BUFS[channels])
                 passes = channels // PAIR
-                nc.sync.dma_start(
-                    out=raw[:].rearrange("p (e x) -> p e x", e=PAIR),
-                    in_=source[0, h, c0 : c0 + channels].rearrange(
-                        "(e c) (a b) v -> (c a) e (b v)", e=PAIR, a=P // passes
-                    ),
-                )
+                for e in range(PAIR):
+                    first = c0 + e * passes
+                    nc.sync.dma_start(
+                        out=raw[:, e * passes * JOINTS : (e + 1) * passes * JOINTS],
+                        in_=source[0, h, first : first + passes].rearrange(
+                            "c (a b) v -> (c a) (b v)", a=P // passes
+                        ),
+                    )
                 chunks.append((raw, r))
         alpha_bf16 = consts.tile([P, HEADS], BF16)
         nc.sync.dma_start(
@@ -82,11 +84,11 @@ def tile_model_pa_kernel(tc, q, k, alphas, att1s, out):
             b = rounds[r][2] // PAIR
             halves = halves_pool.tile([P, 2 * b * JOINTS], BF16, name="halves%d" % b, bufs=BUFS[2 * b])
             to = halves[:].rearrange(
-                "p (b x e i w) -> p x e b i w", b=b, x=2, e=PAIR, i=BLOCKS
+                "p (b x e i w) -> p e x b i w", b=b, x=2, e=PAIR, i=BLOCKS
             )
-            of = raw[:].rearrange("p (e b i x w) -> p x e b i w", b=b, x=2, e=PAIR, i=BLOCKS)
-            for x in range(2):
-                nc.vector.tensor_copy(out=to[:, x], in_=of[:, x])
+            of = raw[:].rearrange("p (e b i x w) -> p e x b i w", b=b, x=2, e=PAIR, i=BLOCKS)
+            for e in range(PAIR):
+                nc.vector.tensor_copy(out=to[:, e], in_=of[:, e])
             halves_of[j] = halves
 
         def transpose(j):
@@ -118,7 +120,7 @@ def tile_model_pa_kernel(tc, q, k, alphas, att1s, out):
                 mx_tiles[r] = (codes, scales)
             codes, scales = mx_tiles[r]
             first = (j % 2) * passes * FRAMES
-            step = min(passes, BURST_PASSES)
+            step = BURST_PASSES if j < len(chunks) - 1 else BURST_PASSES // 2
             for g in range(0, passes, step):
                 columns = slice(first + g * FRAMES, first + (g + step) * FRAMES)
                 nc.vector.quantize_mx(
@@ -137,10 +139,11 @@ def tile_model_pa_kernel(tc, q, k, alphas, att1s, out):
                 scores_of[h] = score_pool.tile([P, MOVING_COLUMNS], F32, name="scores")
             codes, scales = mx_tiles[r]
             for g in range(g0, g1):
-                of_k = slice(g * FRAMES, g * FRAMES + MOVING_COLUMNS)
+                width = MOVING_COLUMNS if r < len(rounds) - 1 else FRAMES
+                of_k = slice(g * FRAMES, g * FRAMES + width)
                 of_q = slice((passes + g) * FRAMES, (passes + g + 1) * FRAMES)
                 nc.tensor.matmul_mx(
-                    out=scores_of[h][:],
+                    out=scores_of[h][:, 0:width],
                     lhsT=codes[:, of_q].bitcast(FP8X4),
                     lhsT_scale=scales[:, of_q],
                     rhs=codes[:, of_k].bitcast(FP8X4),

@@ -16,7 +16,7 @@ FRAMES = 128
 JOINTS = 256
 PAIR = 2
 BLOCK = 32
-BLOCKS = JOINTS // BLOCK
+HALF = BLOCK // 2
 HALF = BLOCK // 2
 ROUND_CHANNELS = ((16, 16), (16, 16), (16, 16), (16, 8, 8))
 BUFS = {16: 4, 8: 4}
@@ -42,7 +42,7 @@ def tile_model_pa_kernel(tc, q, k, alphas, att1s, out):
         ctx.enter_context(tc.manual_schedule())
         consts = ctx.enter_context(tc.tile_pool(name="consts", bufs=1))
         raw_pool = ctx.enter_context(tc.tile_pool(name="raw", bufs=1))
-        halves_pool = ctx.enter_context(tc.tile_pool(name="halves", bufs=1))
+        seconds_pool = ctx.enter_context(tc.tile_pool(name="seconds", bufs=1))
         grouped_pool = ctx.enter_context(tc.tile_pool(name="grouped", bufs=1))
         mx_pool = ctx.enter_context(tc.tile_pool(name="mx", bufs=4))
         result_pool = ctx.enter_context(tc.tile_pool(name="result", bufs=HEADS))
@@ -76,24 +76,23 @@ def tile_model_pa_kernel(tc, q, k, alphas, att1s, out):
         nc.scalar.activation(out=table_warmer[:], in_=identity[:, 0:1], func=mybir.ActivationFunctionType.Tanh)
 
         mx_tiles = {}
-        halves_of = {}
+        seconds_of = {}
         grouped_of = {}
 
-        def split_halves(j):
+        def move(j, e):
             raw, r = chunks[j]
             b = rounds[r][2] // PAIR
-            halves = halves_pool.tile([P, 2 * b * JOINTS], BF16, name="halves%d" % b, bufs=BUFS[2 * b])
-            to = halves[:].rearrange(
-                "p (b x e i w) -> p e x b i w", b=b, x=2, e=PAIR, i=BLOCKS
-            )
-            of = raw[:].rearrange("p (e b i x w) -> p e x b i w", b=b, x=2, e=PAIR, i=BLOCKS)
-            for e in range(PAIR):
-                nc.vector.tensor_copy(out=to[:, e], in_=of[:, e])
-            halves_of[j] = halves
+            if e == 0:
+                seconds_of[j] = seconds_pool.tile([P, b * JOINTS], BF16, name="seconds%d" % b, bufs=BUFS[2 * b])
+            blocks = raw[:].rearrange("p (e n x w) -> p e x n w", e=PAIR, x=2, w=HALF)
+            to = seconds_of[j][:].rearrange("p (n e w) -> p e n w", e=PAIR, w=HALF)
+            nc.vector.tensor_copy(out=to[:, e], in_=blocks[:, e, 1])
+            if e == 1:
+                nc.vector.tensor_copy(out=blocks[:, 0, 1], in_=blocks[:, 1, 0])
 
         def transpose(j):
             passes = rounds[chunks[j][1]][2] // PAIR
-            words = halves_of[j][:].bitcast(F32)
+            words = (chunks[j][0][:].bitcast(F32), seconds_of[j][:].bitcast(F32))
             grouped = grouped_pool.tile(
                 [P, passes * FRAMES * 4], BF16, align_bytes=64, name="grouped%d" % passes, bufs=BUFS[2 * passes]
             )
@@ -103,8 +102,8 @@ def tile_model_pa_kernel(tc, q, k, alphas, att1s, out):
             for i in range(passes // 2):
                 bank = bank_pool.tile([P, 4 * P], F32, name="bank")
                 for n in range(4):
-                    m = (i * 4 + n) * P
-                    nc.tensor.transpose(bank[:, n * P : (n + 1) * P], words[:, m : m + P], identity[:])
+                    m = (i * 2 + n // 2) * P
+                    nc.tensor.transpose(bank[:, n * P : (n + 1) * P], words[n % 2][:, m : m + P], identity[:])
                 nc.scalar.copy(
                     out=grouped_words[:, :, :, i * 4 : (i + 1) * 4],
                     in_=bank[:].rearrange("p (n c a) -> p c a n", n=4, c=passes),
@@ -177,7 +176,8 @@ def tile_model_pa_kernel(tc, q, k, alphas, att1s, out):
         for j in range(-1, steps):
             reached = done[j] if j >= 0 else 0
             while split < steps and done[split] <= reached + AHEAD_CHANNELS:
-                split_halves(split)
+                for e in range(PAIR):
+                    move(split, e)
                 split += 1
             if j >= 0:
                 transpose(j)

@@ -18,9 +18,9 @@ PAIR = 2
 BLOCK = 32
 HALF = BLOCK // 2
 HALF = BLOCK // 2
-ROUND_CHANNELS = ((16, 16), (16, 16), (16, 16), (16, 8, 8))
+ROUND_CHANNELS = ((8, 8, 16), (16, 16), (16, 16), (16, 8, 8))
 BUFS = {16: 4, 8: 4}
-RAW_BUFS = {16: 9, 8: 4}
+RAW_BUFS = {16: 9, 8: 8}
 AHEAD_CHANNELS = 32
 TRANSPOSE_BANKS = 6
 MAX_COLUMNS = 8 * FRAMES

from contextlib import ExitStack

import concourse.mybir as mybir
from concourse.masks import make_identity

F32 = mybir.dt.float32
BF16 = mybir.dt.bfloat16
U32 = mybir.dt.uint32
U8 = mybir.dt.uint8
FP8X4 = mybir.dt.float8_e4m3fn_x4

P = 128
HEADS = 4
CHANNELS = 32
FRAMES = 128
JOINTS = 256
PAIR = 2
BLOCK = 32
HALF = BLOCK // 2
HALF = BLOCK // 2
ROUND_CHANNELS = ((8, 8, 16), (16, 16), (16, 16), (16, 8, 8))
BUFS = {16: 4, 8: 4}
RAW_BUFS = {16: 9, 8: 8}
AHEAD_CHANNELS = 32
TRANSPOSE_BANKS = 6
MAX_COLUMNS = 8 * FRAMES
BURST_PASSES = 4
MOVING_COLUMNS = 256

FLOPS = 2 * HEADS * FRAMES * FRAMES * CHANNELS * JOINTS


def tile_model_pa_kernel(tc, q, k, alphas, att1s, out):
    nc = tc.nc
    rounds = []
    for h in range(HEADS):
        c0 = 0
        for channels in ROUND_CHANNELS[h]:
            rounds.append((h, c0, channels))
            c0 += channels
    with ExitStack() as ctx:
        ctx.enter_context(tc.manual_schedule())
        consts = ctx.enter_context(tc.tile_pool(name="consts", bufs=1))
        raw_pool = ctx.enter_context(tc.tile_pool(name="raw", bufs=1))
        seconds_pool = ctx.enter_context(tc.tile_pool(name="seconds", bufs=1))
        grouped_pool = ctx.enter_context(tc.tile_pool(name="grouped", bufs=1))
        mx_pool = ctx.enter_context(tc.tile_pool(name="mx", bufs=4))
        result_pool = ctx.enter_context(tc.tile_pool(name="result", bufs=HEADS))
        bank_pool = ctx.enter_context(tc.psum_pool(name="banks", bufs=TRANSPOSE_BANKS))
        score_pool = ctx.enter_context(tc.psum_pool(name="scores", bufs=2))

        chunks = []
        for r, (h, c0, channels) in enumerate(rounds):
            for source in (k, q):
                raw = raw_pool.tile([P, channels * JOINTS], BF16, name="raw%d" % channels, bufs=RAW_BUFS[channels])
                passes = channels // PAIR
                for e in range(PAIR):
                    first = c0 + e * passes
                    nc.sync.dma_start(
                        out=raw[:, e * passes * JOINTS : (e + 1) * passes * JOINTS],
                        in_=source[0, h, first : first + passes].rearrange(
                            "c (a b) v -> (c a) (b v)", a=P // passes
                        ),
                    )
                chunks.append((raw, r))
        alpha_bf16 = consts.tile([P, HEADS], BF16)
        nc.sync.dma_start(
            out=alpha_bf16[:], in_=alphas.rearrange("o h x y -> (o h x y)").partition_broadcast(P)
        )
        static_map = consts.tile([P, HEADS, FRAMES], BF16)
        nc.sync.dma_start(out=static_map[:], in_=att1s[0].rearrange("h t u -> t h u"))

        identity = consts.tile([P, P], F32)
        make_identity(nc, identity[:])
        table_warmer = consts.tile([P, 1], F32)
        nc.scalar.activation(out=table_warmer[:], in_=identity[:, 0:1], func=mybir.ActivationFunctionType.Tanh)

        mx_tiles = {}
        seconds_of = {}
        grouped_of = {}

        def move(j, e):
            raw, r = chunks[j]
            b = rounds[r][2] // PAIR
            if e == 0:
                seconds_of[j] = seconds_pool.tile([P, b * JOINTS], BF16, name="seconds%d" % b, bufs=BUFS[2 * b])
            blocks = raw[:].rearrange("p (e n x w) -> p e x n w", e=PAIR, x=2, w=HALF)
            to = seconds_of[j][:].rearrange("p (n e w) -> p e n w", e=PAIR, w=HALF)
            nc.vector.tensor_copy(out=to[:, e], in_=blocks[:, e, 1])
            if e == 1:
                nc.vector.tensor_copy(out=blocks[:, 0, 1], in_=blocks[:, 1, 0])

        def transpose(j):
            passes = rounds[chunks[j][1]][2] // PAIR
            words = (chunks[j][0][:].bitcast(F32), seconds_of[j][:].bitcast(F32))
            grouped = grouped_pool.tile(
                [P, passes * FRAMES * 4], BF16, align_bytes=64, name="grouped%d" % passes, bufs=BUFS[2 * passes]
            )
            grouped_words = grouped[:].bitcast(F32).rearrange(
                "p (c a n) -> p c a n", c=passes, a=P // passes
            )
            for i in range(passes // 2):
                bank = bank_pool.tile([P, 4 * P], F32, name="bank")
                for n in range(4):
                    m = (i * 2 + n // 2) * P
                    nc.tensor.transpose(bank[:, n * P : (n + 1) * P], words[n % 2][:, m : m + P], identity[:])
                nc.scalar.copy(
                    out=grouped_words[:, :, :, i * 4 : (i + 1) * 4],
                    in_=bank[:].rearrange("p (n c a) -> p c a n", n=4, c=passes),
                )
            grouped_of[j] = grouped

        def quantise(j):
            r = chunks[j][1]
            passes = rounds[r][2] // PAIR
            if j % 2 == 0:
                codes = mx_pool.tile([P, 2 * MAX_COLUMNS], U32, align_bytes=64, name="codes")
                scales = mx_pool.tile([P, 2 * MAX_COLUMNS], U8, align_bytes=64, name="scales")
                mx_tiles[r] = (codes, scales)
            codes, scales = mx_tiles[r]
            first = (j % 2) * passes * FRAMES
            step = BURST_PASSES if j < len(chunks) - 1 else BURST_PASSES // 2
            for g in range(0, passes, step):
                columns = slice(first + g * FRAMES, first + (g + step) * FRAMES)
                nc.vector.quantize_mx(
                    out=codes[:, columns].bitcast(FP8X4),
                    scales=scales[:, columns],
                    in_=grouped_of[j][:, g * FRAMES * 4 : (g + step) * FRAMES * 4],
                )

        scores_of = {}
        squashed = {}

        def score_passes(r, g0, g1):
            h, c0, channels = rounds[r]
            passes = channels // PAIR
            if h not in scores_of:
                scores_of[h] = score_pool.tile([P, MOVING_COLUMNS], F32, name="scores")
            codes, scales = mx_tiles[r]
            for g in range(g0, g1):
                width = MOVING_COLUMNS if r < len(rounds) - 1 else FRAMES
                of_k = slice(g * FRAMES, g * FRAMES + width)
                of_q = slice((passes + g) * FRAMES, (passes + g + 1) * FRAMES)
                nc.tensor.matmul_mx(
                    out=scores_of[h][:, 0:width],
                    lhsT=codes[:, of_q].bitcast(FP8X4),
                    lhsT_scale=scales[:, of_q],
                    rhs=codes[:, of_k].bitcast(FP8X4),
                    rhs_scale=scales[:, of_k],
                    start=(c0 == 0 and g == 0),
                    stop=(c0 + channels == CHANNELS and g == passes - 1),
                )

        def squash(h):
            squashed[h] = result_pool.tile([P, FRAMES], F32, name="squashed")
            nc.scalar.activation(
                out=squashed[h][:],
                in_=scores_of[h][:, 0:FRAMES],
                func=mybir.ActivationFunctionType.Tanh,
                scale=1.0 / (CHANNELS * JOINTS),
            )

        steps = len(chunks)
        done = []
        for raw, r in chunks:
            done.append((done[-1] if done else 0) + rounds[r][2])
        to_score = []
        for r in range(len(rounds)):
            passes = rounds[r][2] // PAIR
            for n in range(2):
                to_score.append(
                    (done[2 * r + 1] + AHEAD_CHANNELS + n * 16, r, n * passes // 2, (n + 1) * passes // 2)
                )
        to_squash = []
        split = 0
        for j in range(-1, steps):
            reached = done[j] if j >= 0 else 0
            while split < steps and done[split] <= reached + AHEAD_CHANNELS:
                for e in range(PAIR):
                    move(split, e)
                split += 1
            if j >= 0:
                transpose(j)
                while to_squash:
                    squash(to_squash.pop(0))
                quantise(j)
            while to_score and (to_score[0][0] <= reached or j == steps - 1):
                before, r, g0, g1 = to_score.pop(0)
                score_passes(r, g0, g1)
                h, c0, channels = rounds[r]
                if c0 + channels == CHANNELS and g1 == channels // PAIR:
                    to_squash.append(h)
        while to_squash:
            squash(to_squash.pop(0))

        alpha = consts.tile([P, HEADS], F32)
        nc.vector.tensor_copy(out=alpha[:], in_=alpha_bf16[:])
        for h in range(HEADS):
            result = result_pool.tile([P, FRAMES], F32)
            nc.vector.scalar_tensor_tensor(
                out=result[:],
                in0=squashed[h][:],
                scalar=alpha[:, h : h + 1],
                in1=static_map[:, h, :],
                op0=mybir.AluOpType.mult,
                op1=mybir.AluOpType.add,
            )
            nc.sync.dma_start(out=out[0, h], in_=result[:])
